import numpy as np
import ml_dtypes


def mxq(x, axis, fmt="e4m3"):
    dtype, down = {"e4m3": (ml_dtypes.float8_e4m3fn, 7), "e5m2": (ml_dtypes.float8_e5m2, 14)}[fmt]
    v = np.moveaxis(np.asarray(x, np.float32).astype(ml_dtypes.bfloat16).astype(np.float64), axis, -1)
    blocks = v.reshape(v.shape[:-1] + (-1, 32))
    amax = np.abs(blocks).max(-1, keepdims=True)
    byte = np.maximum(np.where(amax > 0, np.frexp(amax)[1] - 1 + 127, 0) - down, 1)
    scale = np.exp2(byte - 127.0)
    codes = (blocks / scale).astype(np.float32).astype(dtype).astype(np.float64)
    return np.moveaxis((codes * scale).reshape(v.shape), -1, axis)


WIDE = False


def mx_kscale(k):
    if not WIDE:
        return np.ones(k)
    levels = np.array([10, -10, 5, -5, 0])
    if k % 512:
        return np.exp2(np.random.permutation(np.resize(levels, k // 32))).repeat(32)
    a = np.empty((k // 512, 16))
    for p in range(k // 512):
        a[p, :8] = np.random.permutation(np.resize(levels, 8))
        for g in range(8):
            far = levels[np.abs(levels - a[p, g]) >= 10]
            a[p, g + 8] = far[np.random.randint(len(far))]
    return np.exp2(a.ravel()).repeat(32)


BF16 = ml_dtypes.bfloat16


def bf(x):
    return np.asarray(x, np.float32).astype(BF16)


def f64(x):
    return np.asarray(x).astype(np.float64)


B, L, D, O = 2, 256, 512, 16


def setup_inputs():
    s, t = mx_kscale(D), mx_kscale(D)
    return {"input1": bf(np.random.standard_normal((B, L, D)) * s),
            "input2": bf(np.random.standard_normal((B, L, D)) / t),
            "w1": bf(np.random.standard_normal((D, O, D)) * (4.0 / D) / s[:, None, None] * t),
            "aff1": bf(np.random.standard_normal((B, L, O))),
            "aff2": bf(np.random.standard_normal((B, L, O))),
            "bias": bf(1.0 + 0.25 * np.random.standard_normal(O))}


def reference(input1, input2, w1, aff1, aff2, bias):
    u = mxq(f64(input1), 2, "e4m3").reshape(B * L, D) @ mxq(f64(w1), 0, "e4m3").reshape(D, O * D)
    u = u.reshape(B, L * O, D)
    p = mxq(u, 2, "e4m3") @ mxq(f64(input2), 2, "e4m3").transpose(0, 2, 1)
    logits_1 = p.reshape(B, L, O, L).transpose(0, 1, 3, 2)
    logits_2 = f64(aff1)[:, :, None, :] + f64(aff2)[:, None, :, :] + f64(bias)
    return logits_1 + logits_2

@@ -1,0 +1,301 @@
+from contextlib import ExitStack
+
+import concourse.mybir as mybir
+from concourse.masks import make_identity
+
+F32 = mybir.dt.float32
+BF16 = mybir.dt.bfloat16
+U32 = mybir.dt.uint32
+U8 = mybir.dt.uint8
+I32 = mybir.dt.int32
+FP8X4 = mybir.dt.float8_e4m3fn_x4
+ADD = mybir.AluOpType.add
+
+B, L, D, O = 2, 256, 512, 16
+P = 128
+PACK = 4
+NCH = (B * L) // P
+NTOK = B * L
+UNITS = 2 * NCH
+FLOPS = 2 * (B * L) * D * (O * D) + 2 * B * (L * O) * D * L
+
+MANUAL = True
+W_GROUPS = [[0], [1]] + [[o, o + 1] for o in range(2, O, 2)]
+U_GROUPS = [[o, o + 1] for o in range(0, O - 2, 2)] + [[O - 2], [O - 1]]
+W_PREFETCH = 3
+V_EVAC_FROM = 13
+AFFINE_EARLY = 2
+AFFINE_AHEAD = 3
+LAST_SPLIT = 2
+
+
+def tile_biaffine_2_pa_kernel(tc, input1, input2, w1, aff1, aff2, bias, out):
+    nc = tc.nc
+    with ExitStack() as ctx:
+        const = ctx.enter_context(tc.tile_pool(name="const", bufs=1))
+        wraw_pool = ctx.enter_context(tc.tile_pool(name="wraw", bufs=W_PREFETCH))
+        wg_pool = ctx.enter_context(tc.tile_pool(name="wg", bufs=2))
+        wq_pool = ctx.enter_context(tc.tile_pool(name="wq", bufs=3))
+        ug_pool = ctx.enter_context(tc.tile_pool(name="ug", bufs=3))
+        psum = ctx.enter_context(tc.psum_pool(name="psum", bufs=6))
+        psum_c = ctx.enter_context(tc.psum_pool(name="psumc", bufs=2))
+        if MANUAL:
+            ctx.enter_context(tc.manual_schedule())
+
+        ident = const.tile([P, P], BF16)
+        a1pad = const.tile([P, NCH, P], BF16)
+        bias_bc = const.tile([P, O], BF16)
+        sel = const.tile([P, O], BF16)
+        rmat = const.tile([P, L * O], BF16)
+        lmat = const.tile([P, NCH, P], BF16)
+        x1_raw = const.tile([P, NCH, D], BF16)
+        x2_raw = const.tile([P, NCH, D], BF16)
+        x1_g = const.tile([P, NTOK, PACK], BF16, align_bytes=64)
+        x2_g = const.tile([P, NTOK, PACK], BF16, align_bytes=64)
+        x1_c = const.tile([P, NTOK], U32, align_bytes=64)
+        x1_s = const.tile([P, NTOK], U8, align_bytes=64)
+        x2_c = const.tile([P, NTOK], U32, align_bytes=64)
+        x2_s = const.tile([P, NTOK], U8, align_bytes=64)
+        u_c = const.tile([P, O * NTOK], U32, align_bytes=64)
+        u_s = const.tile([P, O * NTOK], U8, align_bytes=64)
+        osb = [const.tile([P, L * O], F32, name="osb%d" % c) for c in range(NCH)]
+
+        w_view = w1.rearrange("(p t) o j -> p t o j", t=PACK)
+        w_raw = {}
+        w_g = {}
+        w_q = {}
+        u_g = {}
+        w_group_of = {}
+        u_group_of = {}
+        for k in range(len(W_GROUPS)):
+            for o in W_GROUPS[k]:
+                w_group_of[o] = k
+        for k in range(len(U_GROUPS)):
+            for o in U_GROUPS[k]:
+                u_group_of[o] = k
+
+        def load_w(k):
+            n = len(W_GROUPS[k])
+            o0 = W_GROUPS[k][0]
+            wr = wraw_pool.tile([P, PACK, 2, D], BF16, name="wr", tag="wr")
+            nc.sync.dma_start(out=wr[:, :, 0:n, :], in_=w_view[:, :, o0:o0 + n, :])
+            w_raw[k] = wr
+
+        def regroup_w(k):
+            if k >= len(W_GROUPS):
+                return
+            n = len(W_GROUPS[k])
+            wg = wg_pool.tile([P, 2 * D, PACK], BF16, name="wg", tag="wg", align_bytes=64)
+            nc.vector.tensor_copy(
+                out=wg[:, 0:n * D, :].rearrange("p (n s m) t -> p n s m t", n=n, s=PACK),
+                in_=w_raw[k][:, :, 0:n, :].rearrange("p t n (m s) -> p n s m t", s=PACK),
+            )
+            w_g[k] = wg
+            if k + W_PREFETCH < len(W_GROUPS):
+                load_w(k + W_PREFETCH)
+
+        def quant_w(k):
+            if k >= len(W_GROUPS):
+                return
+            n = len(W_GROUPS[k])
+            wc = wq_pool.tile([P, 2 * D], U32, name="wc", tag="wc", align_bytes=64)
+            ws = wq_pool.tile([P, 2 * D], U8, name="ws", tag="ws", align_bytes=64)
+            nc.vector.quantize_mx(
+                out=wc[:, 0:n * D].bitcast(FP8X4),
+                scales=ws[:, 0:n * D],
+                in_=w_g[k][:, 0:n * D, :].rearrange("p c t -> p (c t)"),
+            )
+            w_q[k] = (wc, ws)
+
+        def transpose_tokens(raw, grouped, c):
+            xt = psum.tile([P, PACK, P], BF16, name="xt", tag="acc")
+            for t in range(PACK):
+                nc.tensor.transpose(xt[:, t, :], raw[:, c, t:D:PACK], ident[:])
+            nc.scalar.copy(
+                out=grouped[:, c * P:(c + 1) * P, :],
+                in_=xt[:].rearrange("p t r -> p r t"),
+            )
+
+        def quant_tokens(grouped, codes, scales, c0, c1):
+            nc.vector.quantize_mx(
+                out=codes[:, c0 * P:c1 * P].bitcast(FP8X4),
+                scales=scales[:, c0 * P:c1 * P],
+                in_=grouped[:, c0 * P:c1 * P, :].rearrange("p r t -> p (r t)"),
+            )
+
+        def stage1(o):
+            kw = w_group_of[o]
+            wc, ws = w_q[kw]
+            w0 = (o - W_GROUPS[kw][0]) * D
+            ku = u_group_of[o]
+            if o == U_GROUPS[ku][0]:
+                u_g[ku] = ug_pool.tile([P, 2 * NTOK, PACK], BF16, name="ug", tag="ug", align_bytes=64)
+            ug = u_g[ku]
+            r0 = (o - U_GROUPS[ku][0]) * NTOK
+            for c in range(NCH):
+                ub = psum.tile([P, PACK, P], F32, name="ub", tag="acc")
+                for t in range(PACK):
+                    nc.tensor.matmul_mx(
+                        out=ub[:, t, :],
+                        lhsT=wc[:, w0 + t * P:w0 + (t + 1) * P].bitcast(FP8X4),
+                        lhsT_scale=ws[:, w0 + t * P:w0 + (t + 1) * P],
+                        rhs=x1_c[:, c * P:(c + 1) * P].bitcast(FP8X4),
+                        rhs_scale=x1_s[:, c * P:(c + 1) * P],
+                        start=True,
+                        stop=True,
+                    )
+                dst = ug[:, r0 + c * P:r0 + (c + 1) * P, :]
+                src = ub[:].rearrange("p t r -> p r t")
+                if o >= V_EVAC_FROM and c >= 2:
+                    nc.vector.tensor_copy(out=dst, in_=src)
+                else:
+                    nc.scalar.copy(out=dst, in_=src)
+
+        def quant_u(k):
+            n = len(U_GROUPS[k])
+            o0 = U_GROUPS[k][0]
+            nc.vector.quantize_mx(
+                out=u_c[:, o0 * NTOK:(o0 + n) * NTOK].bitcast(FP8X4),
+                scales=u_s[:, o0 * NTOK:(o0 + n) * NTOK],
+                in_=u_g[k][:, 0:n * NTOK, :].rearrange("p r t -> p (r t)"),
+            )
+
+        affine_done = [0]
+
+        def affine_quarters(upto):
+            while affine_done[0] < min(upto, 4 * UNITS):
+                m, q = divmod(affine_done[0], 4)
+                affine_done[0] = affine_done[0] + 1
+                c, yh = divmod(m, 2)
+                s = yh * 4 + q
+                cb = psum_c.tile([P, 512], F32, name="cb", tag="cb")
+                nc.tensor.matmul(
+                    out=cb[:],
+                    lhsT=lmat[:, c, :],
+                    rhs=rmat[:, s * 512:(s + 1) * 512],
+                    start=True,
+                    stop=True,
+                )
+                nc.scalar.copy(out=osb[c][:, s * 512:(s + 1) * 512], in_=cb[:])
+
+        def out_view(m):
+            c, yh = divmod(m, 2)
+            half = L * O // 2
+            return osb[c][:, yh * half:(yh + 1) * half].rearrange("p (y o) -> p y o", o=O)
+
+        def stage2_passes(m, g):
+            c, yh = divmod(m, 2)
+            c2 = 2 * (c // 2) + yh
+            pb = psum.tile([P, 4, P], F32, name="pb", tag="acc")
+            for oo in range(4):
+                u0 = (4 * g + oo) * NTOK + c * P
+                nc.tensor.matmul_mx(
+                    out=pb[:, oo, :],
+                    lhsT=u_c[:, u0:u0 + P].bitcast(FP8X4),
+                    lhsT_scale=u_s[:, u0:u0 + P],
+                    rhs=x2_c[:, c2 * P:(c2 + 1) * P].bitcast(FP8X4),
+                    rhs_scale=x2_s[:, c2 * P:(c2 + 1) * P],
+                    start=True,
+                    stop=True,
+                )
+            return pb
+
+        def final_add(m, g, pb, y0, y1):
+            ov = out_view(m)
+            nc.vector.tensor_tensor(
+                out=ov[:, y0:y1, 4 * g:4 * g + 4],
+                in0=pb[:, :, y0:y1].rearrange("p o y -> p y o"),
+                in1=ov[:, y0:y1, 4 * g:4 * g + 4],
+                op=ADD,
+            )
+
+        def store(m, y0, y1):
+            c, yh = divmod(m, 2)
+            b, h = divmod(c, 2)
+            nc.sync.dma_start(
+                out=out[b, h * P:(h + 1) * P, yh * P + y0:yh * P + y1, :],
+                in_=out_view(m)[:, y0:y1, :],
+            )
+
+        make_identity(nc, ident[:])
+        nc.vector.memset(a1pad[:].bitcast(I32), 0)
+        nc.scalar.dma_start(out=a1pad[:, :, 0:O], in_=aff1.rearrange("b (h p) o -> p (b h) o", p=P))
+        nc.scalar.dma_start(out=bias_bc[:], in_=bias.partition_broadcast(P))
+        load_w(0)
+        nc.sync.dma_start(out=x1_raw[:], in_=input1.rearrange("b (h p) i -> p (b h) i", p=P))
+        for k in range(1, W_PREFETCH):
+            load_w(k)
+        nc.scalar.dma_start(out=x2_raw[:], in_=input2.rearrange("b (h p) i -> p (b h) i", p=P))
+
+        nc.vector.tensor_tensor(out=sel[:], in0=ident[:, 0:O], in1=ident[:, O:2 * O], op=ADD)
+        rview = rmat[:].rearrange("p (y o) -> p y o", o=O)
+        nc.vector.tensor_copy(
+            out=rview[:, 0:L // 2, :],
+            in_=sel[:].unsqueeze(1).to_broadcast([P, L // 2, O]),
+        )
+        nc.scalar.copy(
+            out=rview[:, L // 2:L, :],
+            in_=sel[:].unsqueeze(1).to_broadcast([P, L // 2, O]),
+        )
+        nc.gpsimd.dma_start(out=rmat[2 * O:2 * O + B, :], in_=aff2.rearrange("b y o -> b (y o)"))
+
+        for c in range(NCH):
+            transpose_tokens(x1_raw, x1_g, c)
+        regroup_w(0)
+        quant_w(0)
+        quant_tokens(x1_g, x1_c, x1_s, 0, 1)
+        quant_tokens(x1_g, x1_c, x1_s, 1, 2)
+        regroup_w(1)
+        quant_tokens(x1_g, x1_c, x1_s, 2, 3)
+        quant_tokens(x1_g, x1_c, x1_s, 3, 4)
+        quant_w(1)
+        regroup_w(2)
+
+        for s in range(O):
+            k = s // 2
+            if s == 0:
+                quant_w(2)
+            elif s == 1:
+                regroup_w(3)
+            elif s % 2 == 0:
+                quant_u(k - 1)
+                quant_w(k + 2)
+            else:
+                regroup_w(k + 3)
+            if s == 3:
+                nc.vector.tensor_copy(
+                    out=a1pad[:, :, O:2 * O],
+                    in_=bias_bc[:].unsqueeze(1).to_broadcast([P, NCH, O]),
+                )
+                for b in range(B):
+                    nc.vector.memset(a1pad[:, 2 * b:2 * b + 2, 2 * O + b:2 * O + b + 1], 1.0)
+            if s == 3 or s == 5:
+                transpose_tokens(x2_raw, x2_g, s - 3)
+                transpose_tokens(x2_raw, x2_g, s - 2)
+            if s == 7:
+                quant_tokens(x2_g, x2_c, x2_s, 0, NCH)
+                lt = psum.tile([P, NCH, P], BF16, name="lt", tag="acc")
+                for c in range(NCH):
+                    nc.tensor.transpose(lt[:, c, :], a1pad[:, c, :], ident[:])
+                nc.scalar.copy(out=lmat[:], in_=lt[:])
+            if s == O - 1:
+                quant_u(len(U_GROUPS) - 2)
+                affine_quarters(AFFINE_EARLY)
+            stage1(s)
+        quant_u(len(U_GROUPS) - 1)
+
+        for m in range(UNITS):
+            if m < UNITS - 1:
+                for g in range(4):
+                    affine_quarters(4 * m + g + AFFINE_AHEAD + 1)
+                    pb = stage2_passes(m, g)
+                    final_add(m, g, pb, 0, P)
+                store(m, 0, P)
+            else:
+                affine_quarters(4 * UNITS)
+                banks = [stage2_passes(m, g) for g in range(4)]
+                step = P // LAST_SPLIT
+                for y0 in range(0, P, step):
+                    for g in range(4):
+                        final_add(m, g, banks[g], y0, y0 + step)
+                    store(m, y0, y0 + step)

@@ -10,23 +10,23 @@ U8 = mybir.dt.uint8
 I32 = mybir.dt.int32
 FP8X4 = mybir.dt.float8_e4m3fn_x4
 ADD = mybir.AluOpType.add
+MULT = mybir.AluOpType.mult
 
 B, L, D, O = 2, 256, 512, 16
 P = 128
 PACK = 4
 NCH = (B * L) // P
 NTOK = B * L
-UNITS = 2 * NCH
+QG = 4
+NG = O // QG
+AFF_BUFS = 9
+FIRST = 2
+YQ = 4
 FLOPS = 2 * (B * L) * D * (O * D) + 2 * B * (L * O) * D * L
 
-MANUAL = True
 W_GROUPS = [[0], [1]] + [[o, o + 1] for o in range(2, O, 2)]
-U_GROUPS = [[o, o + 1] for o in range(0, O - 2, 2)] + [[O - 2], [O - 1]]
 W_PREFETCH = 3
-V_EVAC_FROM = 13
-AFFINE_EARLY = 2
-AFFINE_AHEAD = 3
-LAST_SPLIT = 2
+S_SHARE = 6
 
 
 def tile_biaffine_2_pa_kernel(tc, input1, input2, w1, aff1, aff2, bias, out):
@@ -35,84 +35,98 @@ def tile_biaffine_2_pa_kernel(tc, input1, input2, w1, aff1, aff2, bias, out):
         const = ctx.enter_context(tc.tile_pool(name="const", bufs=1))
         wraw_pool = ctx.enter_context(tc.tile_pool(name="wraw", bufs=W_PREFETCH))
         wg_pool = ctx.enter_context(tc.tile_pool(name="wg", bufs=2))
-        wq_pool = ctx.enter_context(tc.tile_pool(name="wq", bufs=3))
-        ug_pool = ctx.enter_context(tc.tile_pool(name="ug", bufs=3))
-        psum = ctx.enter_context(tc.psum_pool(name="psum", bufs=6))
-        psum_c = ctx.enter_context(tc.psum_pool(name="psumc", bufs=2))
-        if MANUAL:
-            ctx.enter_context(tc.manual_schedule())
+        ug_pool = ctx.enter_context(tc.tile_pool(name="ug", bufs=4))
+        uq_pool = ctx.enter_context(tc.tile_pool(name="uq", bufs=9))
+        cp_pool = ctx.enter_context(tc.tile_pool(name="cp", bufs=AFF_BUFS))
+        ob_pool = ctx.enter_context(tc.tile_pool(name="ob", bufs=4))
+        psum_u = ctx.enter_context(tc.psum_pool(name="psumu", bufs=4))
+        psum_o = ctx.enter_context(tc.psum_pool(name="psumo", bufs=4))
+        ctx.enter_context(tc.manual_schedule())
 
+        ident_f = const.tile([P, P], F32)
         ident = const.tile([P, P], BF16)
-        a1pad = const.tile([P, NCH, P], BF16)
+        a1_raw = const.tile([P, NCH, O], BF16)
         bias_bc = const.tile([P, O], BF16)
-        sel = const.tile([P, O], BF16)
-        rmat = const.tile([P, L * O], BF16)
-        lmat = const.tile([P, NCH, P], BF16)
+        a1b = const.tile([P, NCH, O], F32)
+        a2_rows = const.tile([P, L // YQ, O], BF16)
+        a2_perm = const.tile([P, O, L // YQ], BF16)
+        a2t = const.tile([P, B, O, L], BF16)
         x1_raw = const.tile([P, NCH, D], BF16)
         x2_raw = const.tile([P, NCH, D], BF16)
+        x2_perm = const.tile([P, NCH, PACK, P], BF16)
         x1_g = const.tile([P, NTOK, PACK], BF16, align_bytes=64)
         x2_g = const.tile([P, NTOK, PACK], BF16, align_bytes=64)
         x1_c = const.tile([P, NTOK], U32, align_bytes=64)
         x1_s = const.tile([P, NTOK], U8, align_bytes=64)
         x2_c = const.tile([P, NTOK], U32, align_bytes=64)
         x2_s = const.tile([P, NTOK], U8, align_bytes=64)
-        u_c = const.tile([P, O * NTOK], U32, align_bytes=64)
-        u_s = const.tile([P, O * NTOK], U8, align_bytes=64)
-        osb = [const.tile([P, L * O], F32, name="osb%d" % c) for c in range(NCH)]
+        w_c = const.tile([P, O * D], U32, align_bytes=64)
+        w_s = const.tile([P, O * D], U8, align_bytes=64)
 
-        w_view = w1.rearrange("(p t) o j -> p t o j", t=PACK)
+        w_view = w1.rearrange("(p k) o j -> p k o j", k=PACK)
         w_raw = {}
         w_g = {}
-        w_q = {}
         u_g = {}
+        u_q = {}
+        cprime = {}
+        obuf = {}
         w_group_of = {}
-        u_group_of = {}
         for k in range(len(W_GROUPS)):
             for o in W_GROUPS[k]:
                 w_group_of[o] = k
-        for k in range(len(U_GROUPS)):
-            for o in U_GROUPS[k]:
-                u_group_of[o] = k
 
         def load_w(k):
+            if k >= len(W_GROUPS):
+                return
             n = len(W_GROUPS[k])
             o0 = W_GROUPS[k][0]
             wr = wraw_pool.tile([P, PACK, 2, D], BF16, name="wr", tag="wr")
             nc.sync.dma_start(out=wr[:, :, 0:n, :], in_=w_view[:, :, o0:o0 + n, :])
             w_raw[k] = wr
 
-        def regroup_w(k):
+        def interleave_w(k, on_vector, on_scalar):
             if k >= len(W_GROUPS):
                 return
             n = len(W_GROUPS[k])
-            wg = wg_pool.tile([P, 2 * D, PACK], BF16, name="wg", tag="wg", align_bytes=64)
-            nc.vector.tensor_copy(
-                out=wg[:, 0:n * D, :].rearrange("p (n s m) t -> p n s m t", n=n, s=PACK),
-                in_=w_raw[k][:, :, 0:n, :].rearrange("p t n (m s) -> p n s m t", s=PACK),
-            )
-            w_g[k] = wg
-            if k + W_PREFETCH < len(W_GROUPS):
-                load_w(k + W_PREFETCH)
+            if k not in w_g:
+                w_g[k] = wg_pool.tile([P, 2 * D, PACK], BF16, name="wg", tag="wg", align_bytes=64)
+            cut = n * (32 - S_SHARE)
+            dst = w_g[k][:, 0:n * D, :].rearrange("p (t x i) k -> p x t k i", t=PACK, i=4)
+            src = w_raw[k][:, :, 0:n, :].rearrange("p k n (a t i) -> p k (n a) t i", t=PACK, i=4).rearrange(
+                "p k x t i -> p x t k i")
+            if on_vector:
+                nc.vector.tensor_copy(out=dst[:, 0:cut], in_=src[:, 0:cut])
+            if on_scalar:
+                nc.scalar.copy(out=dst[:, cut:n * 32], in_=src[:, cut:n * 32])
 
         def quant_w(k):
             if k >= len(W_GROUPS):
                 return
             n = len(W_GROUPS[k])
-            wc = wq_pool.tile([P, 2 * D], U32, name="wc", tag="wc", align_bytes=64)
-            ws = wq_pool.tile([P, 2 * D], U8, name="ws", tag="ws", align_bytes=64)
+            c0 = W_GROUPS[k][0] * D
             nc.vector.quantize_mx(
-                out=wc[:, 0:n * D].bitcast(FP8X4),
-                scales=ws[:, 0:n * D],
+                out=w_c[:, c0:c0 + n * D].bitcast(FP8X4),
+                scales=w_s[:, c0:c0 + n * D],
                 in_=w_g[k][:, 0:n * D, :].rearrange("p c t -> p (c t)"),
             )
-            w_q[k] = (wc, ws)
 
-        def transpose_tokens(raw, grouped, c):
-            xt = psum.tile([P, PACK, P], BF16, name="xt", tag="acc")
+        def prep_x1(c0, c1, copy):
+            xt = psum_o.tile([P, c1 - c0, 2, P], F32, name="xt", tag="o")
+            for c in range(c0, c1):
+                words = x1_raw[:, c, :].bitcast(F32)
+                for u in range(2):
+                    nc.tensor.transpose(xt[:, c - c0, u, :], words[:, u:D // 2:2], ident_f[:])
+            copy(
+                out=x1_g[:, c0 * P:c1 * P, :].bitcast(F32).rearrange("p (c r) u -> p c r u", r=P),
+                in_=xt[:].rearrange("p c u r -> p c r u"),
+            )
+
+        def prep_x2(c):
+            xt = psum_o.tile([P, PACK, P], BF16, name="xt2", tag="o")
             for t in range(PACK):
-                nc.tensor.transpose(xt[:, t, :], raw[:, c, t:D:PACK], ident[:])
+                nc.tensor.transpose(xt[:, t, :], x2_perm[:, c, t, :], ident[:])
             nc.scalar.copy(
-                out=grouped[:, c * P:(c + 1) * P, :],
+                out=x2_g[:, c * P:(c + 1) * P, :],
                 in_=xt[:].rearrange("p t r -> p r t"),
             )
 
@@ -123,76 +137,81 @@ def tile_biaffine_2_pa_kernel(tc, input1, input2, w1, aff1, aff2, bias, out):
                 in_=grouped[:, c0 * P:c1 * P, :].rearrange("p r t -> p (r t)"),
             )
 
-        def stage1(o):
-            kw = w_group_of[o]
-            wc, ws = w_q[kw]
-            w0 = (o - W_GROUPS[kw][0]) * D
-            ku = u_group_of[o]
-            if o == U_GROUPS[ku][0]:
-                u_g[ku] = ug_pool.tile([P, 2 * NTOK, PACK], BF16, name="ug", tag="ug", align_bytes=64)
-            ug = u_g[ku]
-            r0 = (o - U_GROUPS[ku][0]) * NTOK
-            for c in range(NCH):
-                ub = psum.tile([P, PACK, P], F32, name="ub", tag="acc")
-                for t in range(PACK):
-                    nc.tensor.matmul_mx(
-                        out=ub[:, t, :],
-                        lhsT=wc[:, w0 + t * P:w0 + (t + 1) * P].bitcast(FP8X4),
-                        lhsT_scale=ws[:, w0 + t * P:w0 + (t + 1) * P],
-                        rhs=x1_c[:, c * P:(c + 1) * P].bitcast(FP8X4),
-                        rhs_scale=x1_s[:, c * P:(c + 1) * P],
-                        start=True,
-                        stop=True,
-                    )
-                dst = ug[:, r0 + c * P:r0 + (c + 1) * P, :]
-                src = ub[:].rearrange("p t r -> p r t")
-                if o >= V_EVAC_FROM and c >= 2:
-                    nc.vector.tensor_copy(out=dst, in_=src)
-                else:
-                    nc.scalar.copy(out=dst, in_=src)
-
-        def quant_u(k):
-            n = len(U_GROUPS[k])
-            o0 = U_GROUPS[k][0]
-            nc.vector.quantize_mx(
-                out=u_c[:, o0 * NTOK:(o0 + n) * NTOK].bitcast(FP8X4),
-                scales=u_s[:, o0 * NTOK:(o0 + n) * NTOK],
-                in_=u_g[k][:, 0:n * NTOK, :].rearrange("p r t -> p (r t)"),
-            )
-
-        affine_done = [0]
-
-        def affine_quarters(upto):
-            while affine_done[0] < min(upto, 4 * UNITS):
-                m, q = divmod(affine_done[0], 4)
-                affine_done[0] = affine_done[0] + 1
-                c, yh = divmod(m, 2)
-                s = yh * 4 + q
-                cb = psum_c.tile([P, 512], F32, name="cb", tag="cb")
-                nc.tensor.matmul(
-                    out=cb[:],
-                    lhsT=lmat[:, c, :],
-                    rhs=rmat[:, s * 512:(s + 1) * 512],
+        def stage1(c, o):
+            k = w_group_of[o]
+            n = len(W_GROUPS[k])
+            base = W_GROUPS[k][0] * D + (o - W_GROUPS[k][0]) * P
+            g, oo = divmod(o, QG)
+            if oo == 0:
+                u_g[(c, g)] = ug_pool.tile([P, QG * P, PACK], BF16, name="ug", tag="ug", align_bytes=64)
+            ub = psum_u.tile([P, PACK, P], F32, name="ub", tag="u")
+            for t in range(PACK):
+                w0 = base + t * n * P
+                nc.tensor.matmul_mx(
+                    out=ub[:, t, :],
+                    lhsT=w_c[:, w0:w0 + P].bitcast(FP8X4),
+                    lhsT_scale=w_s[:, w0:w0 + P],
+                    rhs=x1_c[:, c * P:(c + 1) * P].bitcast(FP8X4),
+                    rhs_scale=x1_s[:, c * P:(c + 1) * P],
                     start=True,
                     stop=True,
                 )
-                nc.scalar.copy(out=osb[c][:, s * 512:(s + 1) * 512], in_=cb[:])
+            nc.scalar.copy(
+                out=u_g[(c, g)][:, oo * P:(oo + 1) * P, :],
+                in_=ub[:].rearrange("p t r -> p r t"),
+            )
 
-        def out_view(m):
-            c, yh = divmod(m, 2)
-            half = L * O // 2
-            return osb[c][:, yh * half:(yh + 1) * half].rearrange("p (y o) -> p y o", o=O)
+        def quant_u(c, g):
+            uc = uq_pool.tile([P, QG * P], U32, name="uc", tag="uc", align_bytes=64)
+            us = uq_pool.tile([P, QG * P], U8, name="us", tag="us", align_bytes=64)
+            nc.vector.quantize_mx(
+                out=uc[:].bitcast(FP8X4),
+                scales=us[:],
+                in_=u_g[(c, g)][:].rearrange("p r t -> p (r t)"),
+            )
+            u_q[(c, g)] = (uc, us)
 
-        def stage2_passes(m, g):
-            c, yh = divmod(m, 2)
+        def spread_aff2(r):
+            b, q = divmod(r, YQ)
+            ab = psum_o.tile([P, O, L // YQ], BF16, name="ab", tag="o")
+            for h in range(2):
+                nc.tensor.matmul(
+                    out=ab[:, h * 8:(h + 1) * 8, :],
+                    lhsT=ident[:, r:r + 1].to_broadcast([P, P]),
+                    rhs=a2_perm[:, h * 8:(h + 1) * 8, :],
+                    start=True,
+                    stop=True,
+                )
+            nc.scalar.copy(out=a2t[:, b, :, q * (L // YQ):(q + 1) * (L // YQ)], in_=ab[:])
+
+        groups = [(c, g) for c in range(NCH) for g in range(NG)]
+
+        def affine(i):
+            if i >= len(groups):
+                return
+            c, g = groups[i]
+            ct = cp_pool.tile([P, QG, L], F32, name="ct", tag="ct")
+            for oo in range(QG):
+                o = QG * g + oo
+                nc.gpsimd.tensor_scalar(
+                    out=ct[:, oo, :],
+                    in0=a2t[:, c // 2, o, :],
+                    scalar1=1.0,
+                    scalar2=a1b[:, c, o:o + 1],
+                    op0=MULT,
+                    op1=ADD,
+                )
+            cprime[(c, g)] = ct
+
+        def stage2(c, g, yh):
+            uc, us = u_q[(c, g)]
             c2 = 2 * (c // 2) + yh
-            pb = psum.tile([P, 4, P], F32, name="pb", tag="acc")
-            for oo in range(4):
-                u0 = (4 * g + oo) * NTOK + c * P
+            pb = psum_o.tile([P, QG, P], F32, name="pb", tag="o")
+            for oo in range(QG):
                 nc.tensor.matmul_mx(
                     out=pb[:, oo, :],
-                    lhsT=u_c[:, u0:u0 + P].bitcast(FP8X4),
-                    lhsT_scale=u_s[:, u0:u0 + P],
+                    lhsT=uc[:, oo * P:(oo + 1) * P].bitcast(FP8X4),
+                    lhsT_scale=us[:, oo * P:(oo + 1) * P],
                     rhs=x2_c[:, c2 * P:(c2 + 1) * P].bitcast(FP8X4),
                     rhs_scale=x2_s[:, c2 * P:(c2 + 1) * P],
                     start=True,
@@ -200,102 +219,107 @@ def tile_biaffine_2_pa_kernel(tc, input1, input2, w1, aff1, aff2, bias, out):
                 )
             return pb
 
-        def final_add(m, g, pb, y0, y1):
-            ov = out_view(m)
+        def final_add(c, g, yh, pb):
+            if g == 0:
+                obuf[(c, yh)] = ob_pool.tile([P, P, O], F32, name="ob", tag="ob")
+            ob = obuf[(c, yh)]
             nc.vector.tensor_tensor(
-                out=ov[:, y0:y1, 4 * g:4 * g + 4],
-                in0=pb[:, :, y0:y1].rearrange("p o y -> p y o"),
-                in1=ov[:, y0:y1, 4 * g:4 * g + 4],
+                out=ob[:, :, QG * g:QG * (g + 1)],
+                in0=pb[:].rearrange("p o y -> p y o"),
+                in1=cprime[(c, g)][:, :, yh * P:(yh + 1) * P].rearrange("p o y -> p y o"),
                 op=ADD,
             )
-
-        def store(m, y0, y1):
-            c, yh = divmod(m, 2)
-            b, h = divmod(c, 2)
-            nc.sync.dma_start(
-                out=out[b, h * P:(h + 1) * P, yh * P + y0:yh * P + y1, :],
-                in_=out_view(m)[:, y0:y1, :],
-            )
-
-        make_identity(nc, ident[:])
-        nc.vector.memset(a1pad[:].bitcast(I32), 0)
-        nc.scalar.dma_start(out=a1pad[:, :, 0:O], in_=aff1.rearrange("b (h p) o -> p (b h) o", p=P))
-        nc.scalar.dma_start(out=bias_bc[:], in_=bias.partition_broadcast(P))
-        load_w(0)
-        nc.sync.dma_start(out=x1_raw[:], in_=input1.rearrange("b (h p) i -> p (b h) i", p=P))
-        for k in range(1, W_PREFETCH):
-            load_w(k)
-        nc.scalar.dma_start(out=x2_raw[:], in_=input2.rearrange("b (h p) i -> p (b h) i", p=P))
-
-        nc.vector.tensor_tensor(out=sel[:], in0=ident[:, 0:O], in1=ident[:, O:2 * O], op=ADD)
-        rview = rmat[:].rearrange("p (y o) -> p y o", o=O)
-        nc.vector.tensor_copy(
-            out=rview[:, 0:L // 2, :],
-            in_=sel[:].unsqueeze(1).to_broadcast([P, L // 2, O]),
-        )
-        nc.scalar.copy(
-            out=rview[:, L // 2:L, :],
-            in_=sel[:].unsqueeze(1).to_broadcast([P, L // 2, O]),
-        )
-        nc.gpsimd.dma_start(out=rmat[2 * O:2 * O + B, :], in_=aff2.rearrange("b y o -> b (y o)"))
-
-        for c in range(NCH):
-            transpose_tokens(x1_raw, x1_g, c)
-        regroup_w(0)
-        quant_w(0)
-        quant_tokens(x1_g, x1_c, x1_s, 0, 1)
-        quant_tokens(x1_g, x1_c, x1_s, 1, 2)
-        regroup_w(1)
-        quant_tokens(x1_g, x1_c, x1_s, 2, 3)
-        quant_tokens(x1_g, x1_c, x1_s, 3, 4)
-        quant_w(1)
-        regroup_w(2)
-
-        for s in range(O):
-            k = s // 2
-            if s == 0:
-                quant_w(2)
-            elif s == 1:
-                regroup_w(3)
-            elif s % 2 == 0:
-                quant_u(k - 1)
-                quant_w(k + 2)
-            else:
-                regroup_w(k + 3)
-            if s == 3:
-                nc.vector.tensor_copy(
-                    out=a1pad[:, :, O:2 * O],
-                    in_=bias_bc[:].unsqueeze(1).to_broadcast([P, NCH, O]),
+            if g == NG - 1:
+                b, h = divmod(c, 2)
+                nc.sync.dma_start(
+                    out=out[b, h * P:(h + 1) * P, yh * P:(yh + 1) * P, :],
+                    in_=ob[:],
                 )
-                for b in range(B):
-                    nc.vector.memset(a1pad[:, 2 * b:2 * b + 2, 2 * O + b:2 * O + b + 1], 1.0)
-            if s == 3 or s == 5:
-                transpose_tokens(x2_raw, x2_g, s - 3)
-                transpose_tokens(x2_raw, x2_g, s - 2)
-            if s == 7:
-                quant_tokens(x2_g, x2_c, x2_s, 0, NCH)
-                lt = psum.tile([P, NCH, P], BF16, name="lt", tag="acc")
-                for c in range(NCH):
-                    nc.tensor.transpose(lt[:, c, :], a1pad[:, c, :], ident[:])
-                nc.scalar.copy(out=lmat[:], in_=lt[:])
-            if s == O - 1:
-                quant_u(len(U_GROUPS) - 2)
-                affine_quarters(AFFINE_EARLY)
-            stage1(s)
-        quant_u(len(U_GROUPS) - 1)
 
-        for m in range(UNITS):
-            if m < UNITS - 1:
-                for g in range(4):
-                    affine_quarters(4 * m + g + AFFINE_AHEAD + 1)
-                    pb = stage2_passes(m, g)
-                    final_add(m, g, pb, 0, P)
-                store(m, 0, P)
-            else:
-                affine_quarters(4 * UNITS)
-                banks = [stage2_passes(m, g) for g in range(4)]
-                step = P // LAST_SPLIT
-                for y0 in range(0, P, step):
-                    for g in range(4):
-                        final_add(m, g, banks[g], y0, y0 + step)
-                    store(m, y0, y0 + step)
+        make_identity(nc, ident_f[:])
+        nc.gpsimd.memset(a2_rows[:].rearrange("p y o -> p (y o)").bitcast(I32), 0)
+        x1_view = input1.rearrange("b (h p) i -> p (b h) i", p=P)
+        nc.sync.dma_start(out=x1_raw[:, 0:FIRST, :], in_=x1_view[:, 0:FIRST, :])
+        load_w(0)
+        load_w(1)
+        nc.scalar.dma_start(out=a1_raw[:], in_=aff1.rearrange("b (h p) o -> p (b h) o", p=P))
+        nc.scalar.dma_start(out=bias_bc[:], in_=bias.partition_broadcast(P))
+        load_w(2)
+        nc.sync.dma_start(out=a2_rows[0:B * YQ, :, :], in_=aff2.rearrange("b (q y) o -> (b q) y o", q=YQ))
+        nc.sync.dma_start(out=x1_raw[:, FIRST:NCH, :], in_=x1_view[:, FIRST:NCH, :])
+        nc.sync.dma_start(out=x2_raw[:], in_=input2.rearrange("b (h p) i -> p (b h) i", p=P))
+
+        nc.vector.tensor_copy(out=ident[:], in_=ident_f[:])
+        prep_x1(0, FIRST, nc.vector.tensor_copy)
+        quant_tokens(x1_g, x1_c, x1_s, 0, FIRST)
+        interleave_w(0, True, True)
+        quant_w(0)
+        interleave_w(1, True, True)
+        load_w(3)
+        load_w(4)
+
+        for k in range(len(W_GROUPS)):
+            interleave_w(k + 2, False, True)
+            quant_w(k + 1)
+            interleave_w(k + 2, True, False)
+            load_w(k + 2 + W_PREFETCH)
+            if k == 1:
+                nc.vector.tensor_tensor(
+                    out=a1b[:], in0=a1_raw[:], in1=bias_bc[:].unsqueeze(1).to_broadcast([P, NCH, O]), op=ADD)
+                nc.vector.tensor_copy(out=a2_perm[:], in_=a2_rows[:].rearrange("p y o -> p o y"))
+            if k == 3:
+                nc.vector.tensor_copy(
+                    out=x2_perm[:].rearrange("p c t (a i) -> p c t a i", i=4),
+                    in_=x2_raw[:].rearrange("p c (a t i) -> p c t a i", t=PACK, i=4),
+                )
+            if k in (3, 5, 7):
+                for c in range(FIRST):
+                    quant_u(c, (k - 3) // 2)
+            for o in W_GROUPS[k]:
+                for c in range(FIRST):
+                    stage1(c, o)
+            if k == 2:
+                prep_x1(FIRST, NCH, nc.scalar.copy)
+            if k == 3:
+                quant_tokens(x1_g, x1_c, x1_s, FIRST, NCH)
+            if k == 4:
+                for c in range(NCH):
+                    prep_x2(c)
+            if k == 5:
+                quant_tokens(x2_g, x2_c, x2_s, 0, NCH)
+            if k in (2, 3, 6, 7):
+                r = 2 * (k - 2) if k < 4 else 2 * (k - 4)
+                spread_aff2(r)
+                spread_aff2(r + 1)
+            if k == 3:
+                for i in range(FIRST * NG):
+                    affine(i)
+            if k == 7:
+                affine(FIRST * NG)
+        for c in range(FIRST):
+            quant_u(c, NG - 1)
+
+        done = 0
+        last = NCH * NG - 1
+        for s in range(FIRST * NG, NCH * NG):
+            c, g = divmod(s, NG)
+            if s > FIRST * NG:
+                quant_u(*groups[s - 1])
+            upto = min(2 * (s - FIRST * NG + 1), s - 1)
+            jobs = [(cc, gg, yh) for cc, gg in groups[done:upto] for yh in range(2)]
+            banks = []
+            for i in range(QG):
+                if i < len(jobs):
+                    banks.append(stage2(*jobs[i]))
+                stage1(c, QG * g + i)
+            for i in range(len(jobs)):
+                final_add(*jobs[i], banks[i])
+            for i in range(done, upto):
+                affine(i + AFF_BUFS)
+            done = upto
+        for cc, gg in groups[done:last]:
+            for yh in range(2):
+                final_add(cc, gg, yh, stage2(cc, gg, yh))
+        quant_u(*groups[last])
+        for yh in range(2):
+            final_add(*groups[last], yh, stage2(*groups[last], yh))

@@ -11,6 +11,7 @@ I32 = mybir.dt.int32
 FP8X4 = mybir.dt.float8_e4m3fn_x4
 ADD = mybir.AluOpType.add
 MULT = mybir.AluOpType.mult
+IDENTITY = mybir.ActivationFunctionType.Identity
 
 B, L, D, O = 2, 256, 512, 16
 P = 128
@@ -20,6 +21,7 @@ NTOK = B * L
 QG = 4
 NG = O // QG
 AFF_BUFS = 9
+V_AFFINE = 2
 FIRST = 2
 YQ = 4
 FLOPS = 2 * (B * L) * D * (O * D) + 2 * B * (L * O) * D * L
@@ -184,23 +186,31 @@ def tile_biaffine_2_pa_kernel(tc, input1, input2, w1, aff1, aff2, bias, out):
                 )
             nc.scalar.copy(out=a2t[:, b, :, q * (L // YQ):(q + 1) * (L // YQ)], in_=ab[:])
 
+        def vector_affine(dst, a2, a1):
+            nc.vector.tensor_scalar(out=dst, in0=a2, scalar1=a1, scalar2=None, op0=ADD)
+
+        def scalar_affine(dst, a2, a1):
+            nc.scalar.activation(out=dst, in_=a2, func=IDENTITY, bias=a1, scale=1.0)
+
+        def gpsimd_affine(dst, a2, a1):
+            nc.gpsimd.tensor_scalar(out=dst, in0=a2, scalar1=1.0, scalar2=a1, op0=MULT, op1=ADD)
+
         groups = [(c, g) for c in range(NCH) for g in range(NG)]
 
         def affine(i):
             if i >= len(groups):
                 return
             c, g = groups[i]
+            if i < V_AFFINE:
+                make = vector_affine
+            elif i % 3 == 0 and i < len(groups) - 1:
+                make = scalar_affine
+            else:
+                make = gpsimd_affine
             ct = cp_pool.tile([P, QG, L], F32, name="ct", tag="ct")
             for oo in range(QG):
                 o = QG * g + oo
-                nc.gpsimd.tensor_scalar(
-                    out=ct[:, oo, :],
-                    in0=a2t[:, c // 2, o, :],
-                    scalar1=1.0,
-                    scalar2=a1b[:, c, o:o + 1],
-                    op0=MULT,
-                    op1=ADD,
-                )
+                make(ct[:, oo, :], a2t[:, c // 2, o, :], a1b[:, c, o:o + 1])
             cprime[(c, g)] = ct
 
         def stage2(c, g, yh):
@@ -258,14 +268,13 @@ def tile_biaffine_2_pa_kernel(tc, input1, input2, w1, aff1, aff2, bias, out):
         load_w(3)
         load_w(4)
 
+        aff2_row = [0]
         for k in range(len(W_GROUPS)):
             interleave_w(k + 2, False, True)
             quant_w(k + 1)
             interleave_w(k + 2, True, False)
             load_w(k + 2 + W_PREFETCH)
             if k == 1:
-                nc.vector.tensor_tensor(
-                    out=a1b[:], in0=a1_raw[:], in1=bias_bc[:].unsqueeze(1).to_broadcast([P, NCH, O]), op=ADD)
                 nc.vector.tensor_copy(out=a2_perm[:], in_=a2_rows[:].rearrange("p y o -> p o y"))
             if k == 3:
                 nc.vector.tensor_copy(
@@ -287,17 +296,17 @@ def tile_biaffine_2_pa_kernel(tc, input1, input2, w1, aff1, aff2, bias, out):
                     prep_x2(c)
             if k == 5:
                 quant_tokens(x2_g, x2_c, x2_s, 0, NCH)
-            if k in (2, 3, 6, 7):
-                r = 2 * (k - 2) if k < 4 else 2 * (k - 4)
-                spread_aff2(r)
-                spread_aff2(r + 1)
-            if k == 3:
-                for i in range(FIRST * NG):
-                    affine(i)
-            if k == 7:
-                affine(FIRST * NG)
+            if 2 <= k < 2 + B * YQ // 2 + 2 and k != 4 and k != 3:
+                for r in range(2):
+                    spread_aff2(aff2_row[0])
+                    aff2_row[0] += 1
+            if k == len(W_GROUPS) - 1:
+                nc.vector.tensor_tensor(
+                    out=a1b[:], in0=a1_raw[:], in1=bias_bc[:].unsqueeze(1).to_broadcast([P, NCH, O]), op=ADD)
         for c in range(FIRST):
             quant_u(c, NG - 1)
+        for i in range(V_AFFINE + 1):
+            affine(i)
 
         done = 0
         last = NCH * NG - 1
@@ -314,8 +323,8 @@ def tile_biaffine_2_pa_kernel(tc, input1, input2, w1, aff1, aff2, bias, out):
                 stage1(c, QG * g + i)
             for i in range(len(jobs)):
                 final_add(*jobs[i], banks[i])
-            for i in range(done, upto):
-                affine(i + AFF_BUFS)
+            affine(V_AFFINE + 1 + 2 * (s - FIRST * NG))
+            affine(V_AFFINE + 2 + 2 * (s - FIRST * NG))
             done = upto
         for cc, gg in groups[done:last]:
             for yh in range(2):

@@ -20,7 +20,9 @@ NCH = (B * L) // P
 NTOK = B * L
 QG = 4
 NG = O // QG
-AFF_BUFS = 9
+AFF_BUFS = 7
+V_EVAC_FROM = 12
+LAST_SPLIT = 2
 V_AFFINE = 2
 FIRST = 2
 YQ = 4
@@ -28,7 +30,7 @@ FLOPS = 2 * (B * L) * D * (O * D) + 2 * B * (L * O) * D * L
 
 W_GROUPS = [[0], [1]] + [[o, o + 1] for o in range(2, O, 2)]
 W_PREFETCH = 3
-S_SHARE = 6
+S_SHARE = 4
 
 
 def tile_biaffine_2_pa_kernel(tc, input1, input2, w1, aff1, aff2, bias, out):
@@ -36,9 +38,9 @@ def tile_biaffine_2_pa_kernel(tc, input1, input2, w1, aff1, aff2, bias, out):
     with ExitStack() as ctx:
         const = ctx.enter_context(tc.tile_pool(name="const", bufs=1))
         wraw_pool = ctx.enter_context(tc.tile_pool(name="wraw", bufs=W_PREFETCH))
-        wg_pool = ctx.enter_context(tc.tile_pool(name="wg", bufs=2))
+        wg_pool = ctx.enter_context(tc.tile_pool(name="wg", bufs=3))
         ug_pool = ctx.enter_context(tc.tile_pool(name="ug", bufs=4))
-        uq_pool = ctx.enter_context(tc.tile_pool(name="uq", bufs=9))
+        uq_pool = ctx.enter_context(tc.tile_pool(name="uq", bufs=8))
         cp_pool = ctx.enter_context(tc.tile_pool(name="cp", bufs=AFF_BUFS))
         ob_pool = ctx.enter_context(tc.tile_pool(name="ob", bufs=4))
         psum_u = ctx.enter_context(tc.psum_pool(name="psumu", bufs=4))
@@ -139,13 +141,10 @@ def tile_biaffine_2_pa_kernel(tc, input1, input2, w1, aff1, aff2, bias, out):
                 in_=grouped[:, c0 * P:c1 * P, :].rearrange("p r t -> p (r t)"),
             )
 
-        def stage1(c, o):
+        def first_product(c, o):
             k = w_group_of[o]
             n = len(W_GROUPS[k])
             base = W_GROUPS[k][0] * D + (o - W_GROUPS[k][0]) * P
-            g, oo = divmod(o, QG)
-            if oo == 0:
-                u_g[(c, g)] = ug_pool.tile([P, QG * P, PACK], BF16, name="ug", tag="ug", align_bytes=64)
             ub = psum_u.tile([P, PACK, P], F32, name="ub", tag="u")
             for t in range(PACK):
                 w0 = base + t * n * P
@@ -158,7 +157,13 @@ def tile_biaffine_2_pa_kernel(tc, input1, input2, w1, aff1, aff2, bias, out):
                     start=True,
                     stop=True,
                 )
-            nc.scalar.copy(
+            return ub
+
+        def take_u(c, o, ub, copy):
+            g, oo = divmod(o, QG)
+            if oo == 0:
+                u_g[(c, g)] = ug_pool.tile([P, QG * P, PACK], BF16, name="ug", tag="ug", align_bytes=64)
+            copy(
                 out=u_g[(c, g)][:, oo * P:(oo + 1) * P, :],
                 in_=ub[:].rearrange("p t r -> p r t"),
             )
@@ -203,7 +208,7 @@ def tile_biaffine_2_pa_kernel(tc, input1, input2, w1, aff1, aff2, bias, out):
             c, g = groups[i]
             if i < V_AFFINE:
                 make = vector_affine
-            elif i % 3 == 0 and i < len(groups) - 1:
+            elif i % 3 == 0 and 3 < i < len(groups) - 1:
                 make = scalar_affine
             else:
                 make = gpsimd_affine
@@ -229,51 +234,56 @@ def tile_biaffine_2_pa_kernel(tc, input1, input2, w1, aff1, aff2, bias, out):
                 )
             return pb
 
-        def final_add(c, g, yh, pb):
+        def final_add(c, g, yh, pb, pieces=1):
             if g == 0:
                 obuf[(c, yh)] = ob_pool.tile([P, P, O], F32, name="ob", tag="ob")
             ob = obuf[(c, yh)]
-            nc.vector.tensor_tensor(
-                out=ob[:, :, QG * g:QG * (g + 1)],
-                in0=pb[:].rearrange("p o y -> p y o"),
-                in1=cprime[(c, g)][:, :, yh * P:(yh + 1) * P].rearrange("p o y -> p y o"),
-                op=ADD,
-            )
-            if g == NG - 1:
-                b, h = divmod(c, 2)
-                nc.sync.dma_start(
-                    out=out[b, h * P:(h + 1) * P, yh * P:(yh + 1) * P, :],
-                    in_=ob[:],
+            step = P // pieces
+            for y0 in range(0, P, step):
+                nc.vector.tensor_tensor(
+                    out=ob[:, y0:y0 + step, QG * g:QG * (g + 1)],
+                    in0=pb[:, :, y0:y0 + step].rearrange("p o y -> p y o"),
+                    in1=cprime[(c, g)][:, :, yh * P + y0:yh * P + y0 + step].rearrange("p o y -> p y o"),
+                    op=ADD,
                 )
+                if g == NG - 1:
+                    b, h = divmod(c, 2)
+                    nc.sync.dma_start(
+                        out=out[b, h * P:(h + 1) * P, yh * P + y0:yh * P + y0 + step, :],
+                        in_=ob[:, y0:y0 + step, :],
+                    )
 
         make_identity(nc, ident_f[:])
         nc.gpsimd.memset(a2_rows[:].rearrange("p y o -> p (y o)").bitcast(I32), 0)
         x1_view = input1.rearrange("b (h p) i -> p (b h) i", p=P)
-        nc.sync.dma_start(out=x1_raw[:, 0:FIRST, :], in_=x1_view[:, 0:FIRST, :])
         load_w(0)
+        nc.sync.dma_start(out=x1_raw[:, 0:FIRST, :], in_=x1_view[:, 0:FIRST, :])
         load_w(1)
+        load_w(2)
         nc.scalar.dma_start(out=a1_raw[:], in_=aff1.rearrange("b (h p) o -> p (b h) o", p=P))
         nc.scalar.dma_start(out=bias_bc[:], in_=bias.partition_broadcast(P))
-        load_w(2)
         nc.sync.dma_start(out=a2_rows[0:B * YQ, :, :], in_=aff2.rearrange("b (q y) o -> (b q) y o", q=YQ))
-        nc.sync.dma_start(out=x1_raw[:, FIRST:NCH, :], in_=x1_view[:, FIRST:NCH, :])
-        nc.sync.dma_start(out=x2_raw[:], in_=input2.rearrange("b (h p) i -> p (b h) i", p=P))
 
         nc.vector.tensor_copy(out=ident[:], in_=ident_f[:])
-        prep_x1(0, FIRST, nc.vector.tensor_copy)
-        quant_tokens(x1_g, x1_c, x1_s, 0, FIRST)
         interleave_w(0, True, True)
-        quant_w(0)
-        interleave_w(1, True, True)
         load_w(3)
+        prep_x1(0, FIRST, nc.scalar.copy)
+        nc.sync.dma_start(out=x1_raw[:, FIRST:NCH, :], in_=x1_view[:, FIRST:NCH, :])
+        interleave_w(1, True, True)
         load_w(4)
+        nc.sync.dma_start(out=x2_raw[:], in_=input2.rearrange("b (h p) i -> p (b h) i", p=P))
+        quant_w(0)
+        quant_tokens(x1_g, x1_c, x1_s, 0, FIRST)
+        interleave_w(2, True, True)
+        load_w(5)
 
         aff2_row = [0]
+        jobs = [(c, g, yh) for c in range(NCH) for g in range(NG) for yh in range(2)]
         for k in range(len(W_GROUPS)):
-            interleave_w(k + 2, False, True)
+            interleave_w(k + 3, False, True)
             quant_w(k + 1)
-            interleave_w(k + 2, True, False)
-            load_w(k + 2 + W_PREFETCH)
+            interleave_w(k + 3, True, False)
+            load_w(k + 3 + W_PREFETCH)
             if k == 1:
                 nc.vector.tensor_copy(out=a2_perm[:], in_=a2_rows[:].rearrange("p y o -> p o y"))
             if k == 3:
@@ -284,9 +294,11 @@ def tile_biaffine_2_pa_kernel(tc, input1, input2, w1, aff1, aff2, bias, out):
             if k in (3, 5, 7):
                 for c in range(FIRST):
                     quant_u(c, (k - 3) // 2)
+            if k == len(W_GROUPS) - 1:
+                early = {job: stage2(*job) for job in jobs[0:4]}
             for o in W_GROUPS[k]:
                 for c in range(FIRST):
-                    stage1(c, o)
+                    take_u(c, o, first_product(c, o), nc.scalar.copy)
             if k == 2:
                 prep_x1(FIRST, NCH, nc.scalar.copy)
             if k == 3:
@@ -296,39 +308,46 @@ def tile_biaffine_2_pa_kernel(tc, input1, input2, w1, aff1, aff2, bias, out):
                     prep_x2(c)
             if k == 5:
                 quant_tokens(x2_g, x2_c, x2_s, 0, NCH)
-            if 2 <= k < 2 + B * YQ // 2 + 2 and k != 4 and k != 3:
+            if k in (2, 5, 6, 7):
                 for r in range(2):
                     spread_aff2(aff2_row[0])
                     aff2_row[0] += 1
-            if k == len(W_GROUPS) - 1:
-                nc.vector.tensor_tensor(
-                    out=a1b[:], in0=a1_raw[:], in1=bias_bc[:].unsqueeze(1).to_broadcast([P, NCH, O]), op=ADD)
+        nc.vector.tensor_tensor(
+            out=a1b[:], in0=a1_raw[:], in1=bias_bc[:].unsqueeze(1).to_broadcast([P, NCH, O]), op=ADD)
+
+        last = NCH * NG - 1
+        done = 0
+        for i in range(4):
+            affine(i)
+        for job in jobs[0:4]:
+            final_add(*job, early[job])
+        done = 4
         for c in range(FIRST):
             quant_u(c, NG - 1)
-        for i in range(V_AFFINE + 1):
-            affine(i)
-
-        done = 0
-        last = NCH * NG - 1
         for s in range(FIRST * NG, NCH * NG):
             c, g = divmod(s, NG)
             if s > FIRST * NG:
                 quant_u(*groups[s - 1])
-            upto = min(2 * (s - FIRST * NG + 1), s - 1)
-            jobs = [(cc, gg, yh) for cc, gg in groups[done:upto] for yh in range(2)]
+            upto = min(done + 4, 2 * (s - 1))
+            now = jobs[done:upto]
             banks = []
             for i in range(QG):
-                if i < len(jobs):
-                    banks.append(stage2(*jobs[i]))
-                stage1(c, QG * g + i)
-            for i in range(len(jobs)):
-                final_add(*jobs[i], banks[i])
-            affine(V_AFFINE + 1 + 2 * (s - FIRST * NG))
-            affine(V_AFFINE + 2 + 2 * (s - FIRST * NG))
+                if i < len(now):
+                    banks.append(stage2(*now[i]))
+                ub = first_product(c, QG * g + i)
+                if i == QG - 1 and s >= V_EVAC_FROM:
+                    late = ub
+                else:
+                    take_u(c, QG * g + i, ub, nc.scalar.copy)
+            for i in range(len(now)):
+                final_add(*now[i], banks[i])
+            if s >= V_EVAC_FROM:
+                take_u(c, QG * g + QG - 1, late, nc.vector.tensor_copy)
+            affine(4 + 2 * (s - FIRST * NG))
+            affine(5 + 2 * (s - FIRST * NG))
             done = upto
-        for cc, gg in groups[done:last]:
-            for yh in range(2):
-                final_add(cc, gg, yh, stage2(cc, gg, yh))
         quant_u(*groups[last])
         for yh in range(2):
-            final_add(*groups[last], yh, stage2(*groups[last], yh))
+            tail = [(NCH - 1, g, yh) for g in range(NG) if (NCH - 1, g, yh) in jobs[done:]]
+            for job in tail:
+                final_add(*job, stage2(*job), LAST_SPLIT if job == jobs[-1] else 1)

@@ -10,8 +10,6 @@ U8 = mybir.dt.uint8
 I32 = mybir.dt.int32
 FP8X4 = mybir.dt.float8_e4m3fn_x4
 ADD = mybir.AluOpType.add
-MULT = mybir.AluOpType.mult
-IDENTITY = mybir.ActivationFunctionType.Identity
 
 B, L, D, O = 2, 256, 512, 16
 P = 128
@@ -20,17 +18,16 @@ NCH = (B * L) // P
 NTOK = B * L
 QG = 4
 NG = O // QG
-AFF_BUFS = 7
-V_EVAC_FROM = 12
+EARLY = 3
+V_EVAC_FROM = 14
 LAST_SPLIT = 2
-V_AFFINE = 2
+C_HEAD = 4
+C_STEP = 2
 FIRST = 2
-YQ = 4
 FLOPS = 2 * (B * L) * D * (O * D) + 2 * B * (L * O) * D * L
 
 W_GROUPS = [[0], [1]] + [[o, o + 1] for o in range(2, O, 2)]
 W_PREFETCH = 3
-S_SHARE = 4
 
 
 def tile_biaffine_2_pa_kernel(tc, input1, input2, w1, aff1, aff2, bias, out):
@@ -41,20 +38,19 @@ def tile_biaffine_2_pa_kernel(tc, input1, input2, w1, aff1, aff2, bias, out):
         wg_pool = ctx.enter_context(tc.tile_pool(name="wg", bufs=3))
         ug_pool = ctx.enter_context(tc.tile_pool(name="ug", bufs=4))
         uq_pool = ctx.enter_context(tc.tile_pool(name="uq", bufs=8))
-        cp_pool = ctx.enter_context(tc.tile_pool(name="cp", bufs=AFF_BUFS))
-        ob_pool = ctx.enter_context(tc.tile_pool(name="ob", bufs=4))
-        psum_u = ctx.enter_context(tc.psum_pool(name="psumu", bufs=4))
-        psum_o = ctx.enter_context(tc.psum_pool(name="psumo", bufs=4))
+        psum_u = ctx.enter_context(tc.psum_pool(name="psumu", bufs=3))
+        psum_o = ctx.enter_context(tc.psum_pool(name="psumo", bufs=3))
+        psum_c = ctx.enter_context(tc.psum_pool(name="psumc", bufs=2))
         ctx.enter_context(tc.manual_schedule())
 
         ident_f = const.tile([P, P], F32)
         ident = const.tile([P, P], BF16)
         a1_raw = const.tile([P, NCH, O], BF16)
+        a1pad = const.tile([P, NCH, P], BF16)
         bias_bc = const.tile([P, O], BF16)
-        a1b = const.tile([P, NCH, O], F32)
-        a2_rows = const.tile([P, L // YQ, O], BF16)
-        a2_perm = const.tile([P, O, L // YQ], BF16)
-        a2t = const.tile([P, B, O, L], BF16)
+        sel = const.tile([P, O], BF16)
+        rmat = const.tile([P, L * O], BF16)
+        lmat = const.tile([P, NCH, P], BF16)
         x1_raw = const.tile([P, NCH, D], BF16)
         x2_raw = const.tile([P, NCH, D], BF16)
         x2_perm = const.tile([P, NCH, PACK, P], BF16)
@@ -66,14 +62,13 @@ def tile_biaffine_2_pa_kernel(tc, input1, input2, w1, aff1, aff2, bias, out):
         x2_s = const.tile([P, NTOK], U8, align_bytes=64)
         w_c = const.tile([P, O * D], U32, align_bytes=64)
         w_s = const.tile([P, O * D], U8, align_bytes=64)
+        osb = [const.tile([P, L, O], F32, name="osb%d" % c) for c in range(NCH)]
 
         w_view = w1.rearrange("(p k) o j -> p k o j", k=PACK)
         w_raw = {}
         w_g = {}
         u_g = {}
         u_q = {}
-        cprime = {}
-        obuf = {}
         w_group_of = {}
         for k in range(len(W_GROUPS)):
             for o in W_GROUPS[k]:
@@ -88,20 +83,17 @@ def tile_biaffine_2_pa_kernel(tc, input1, input2, w1, aff1, aff2, bias, out):
             nc.sync.dma_start(out=wr[:, :, 0:n, :], in_=w_view[:, :, o0:o0 + n, :])
             w_raw[k] = wr
 
-        def interleave_w(k, on_vector, on_scalar):
+        def interleave_w(k):
             if k >= len(W_GROUPS):
                 return
             n = len(W_GROUPS[k])
-            if k not in w_g:
-                w_g[k] = wg_pool.tile([P, 2 * D, PACK], BF16, name="wg", tag="wg", align_bytes=64)
-            cut = n * (32 - S_SHARE)
-            dst = w_g[k][:, 0:n * D, :].rearrange("p (t x i) k -> p x t k i", t=PACK, i=4)
-            src = w_raw[k][:, :, 0:n, :].rearrange("p k n (a t i) -> p k (n a) t i", t=PACK, i=4).rearrange(
-                "p k x t i -> p x t k i")
-            if on_vector:
-                nc.vector.tensor_copy(out=dst[:, 0:cut], in_=src[:, 0:cut])
-            if on_scalar:
-                nc.scalar.copy(out=dst[:, cut:n * 32], in_=src[:, cut:n * 32])
+            w_g[k] = wg_pool.tile([P, 2 * D, PACK], BF16, name="wg", tag="wg", align_bytes=64)
+            nc.vector.tensor_copy(
+                out=w_g[k][:, 0:n * D, :].rearrange("p (t x i) k -> p x t k i", t=PACK, i=4),
+                in_=w_raw[k][:, :, 0:n, :].rearrange("p k n (a t i) -> p k (n a) t i", t=PACK, i=4).rearrange(
+                    "p k x t i -> p x t k i"),
+            )
+            load_w(k + W_PREFETCH)
 
         def quant_w(k):
             if k >= len(W_GROUPS):
@@ -178,45 +170,22 @@ def tile_biaffine_2_pa_kernel(tc, input1, input2, w1, aff1, aff2, bias, out):
             )
             u_q[(c, g)] = (uc, us)
 
-        def spread_aff2(r):
-            b, q = divmod(r, YQ)
-            ab = psum_o.tile([P, O, L // YQ], BF16, name="ab", tag="o")
-            for h in range(2):
+        groups = [(c, g) for c in range(NCH) for g in range(NG)]
+        affine_done = [0]
+
+        def affine_banks(upto):
+            while affine_done[0] < min(upto, NCH * 8):
+                c, s = divmod(affine_done[0], 8)
+                affine_done[0] = affine_done[0] + 1
+                cb = psum_c.tile([P, 32, O], F32, name="cb", tag="cb")
                 nc.tensor.matmul(
-                    out=ab[:, h * 8:(h + 1) * 8, :],
-                    lhsT=ident[:, r:r + 1].to_broadcast([P, P]),
-                    rhs=a2_perm[:, h * 8:(h + 1) * 8, :],
+                    out=cb[:],
+                    lhsT=lmat[:, c, :],
+                    rhs=rmat[:, s * 512:(s + 1) * 512],
                     start=True,
                     stop=True,
                 )
-            nc.scalar.copy(out=a2t[:, b, :, q * (L // YQ):(q + 1) * (L // YQ)], in_=ab[:])
-
-        def vector_affine(dst, a2, a1):
-            nc.vector.tensor_scalar(out=dst, in0=a2, scalar1=a1, scalar2=None, op0=ADD)
-
-        def scalar_affine(dst, a2, a1):
-            nc.scalar.activation(out=dst, in_=a2, func=IDENTITY, bias=a1, scale=1.0)
-
-        def gpsimd_affine(dst, a2, a1):
-            nc.gpsimd.tensor_scalar(out=dst, in0=a2, scalar1=1.0, scalar2=a1, op0=MULT, op1=ADD)
-
-        groups = [(c, g) for c in range(NCH) for g in range(NG)]
-
-        def affine(i):
-            if i >= len(groups):
-                return
-            c, g = groups[i]
-            if i < V_AFFINE:
-                make = vector_affine
-            elif i % 3 == 0 and 3 < i < len(groups) - 1:
-                make = scalar_affine
-            else:
-                make = gpsimd_affine
-            ct = cp_pool.tile([P, QG, L], F32, name="ct", tag="ct")
-            for oo in range(QG):
-                o = QG * g + oo
-                make(ct[:, oo, :], a2t[:, c // 2, o, :], a1b[:, c, o:o + 1])
-            cprime[(c, g)] = ct
+                nc.scalar.copy(out=osb[c][:, s * 32:(s + 1) * 32, :], in_=cb[:])
 
         def stage2(c, g, yh):
             uc, us = u_q[(c, g)]
@@ -235,15 +204,13 @@ def tile_biaffine_2_pa_kernel(tc, input1, input2, w1, aff1, aff2, bias, out):
             return pb
 
         def final_add(c, g, yh, pb, pieces=1):
-            if g == 0:
-                obuf[(c, yh)] = ob_pool.tile([P, P, O], F32, name="ob", tag="ob")
-            ob = obuf[(c, yh)]
+            ob = osb[c][:, yh * P:(yh + 1) * P, :]
             step = P // pieces
             for y0 in range(0, P, step):
                 nc.vector.tensor_tensor(
                     out=ob[:, y0:y0 + step, QG * g:QG * (g + 1)],
                     in0=pb[:, :, y0:y0 + step].rearrange("p o y -> p y o"),
-                    in1=cprime[(c, g)][:, :, yh * P + y0:yh * P + y0 + step].rearrange("p o y -> p y o"),
+                    in1=ob[:, y0:y0 + step, QG * g:QG * (g + 1)],
                     op=ADD,
                 )
                 if g == NG - 1:
@@ -254,38 +221,45 @@ def tile_biaffine_2_pa_kernel(tc, input1, input2, w1, aff1, aff2, bias, out):
                     )
 
         make_identity(nc, ident_f[:])
-        nc.gpsimd.memset(a2_rows[:].rearrange("p y o -> p (y o)").bitcast(I32), 0)
         x1_view = input1.rearrange("b (h p) i -> p (b h) i", p=P)
+        nc.scalar.dma_start(out=a1_raw[:], in_=aff1.rearrange("b (h p) o -> p (b h) o", p=P))
+        nc.scalar.dma_start(out=bias_bc[:], in_=bias.partition_broadcast(P))
         load_w(0)
         nc.sync.dma_start(out=x1_raw[:, 0:FIRST, :], in_=x1_view[:, 0:FIRST, :])
         load_w(1)
-        load_w(2)
-        nc.scalar.dma_start(out=a1_raw[:], in_=aff1.rearrange("b (h p) o -> p (b h) o", p=P))
-        nc.scalar.dma_start(out=bias_bc[:], in_=bias.partition_broadcast(P))
-        nc.sync.dma_start(out=a2_rows[0:B * YQ, :, :], in_=aff2.rearrange("b (q y) o -> (b q) y o", q=YQ))
-
+        nc.vector.memset(a1pad[:].bitcast(I32), 0)
         nc.vector.tensor_copy(out=ident[:], in_=ident_f[:])
-        interleave_w(0, True, True)
-        load_w(3)
-        prep_x1(0, FIRST, nc.scalar.copy)
-        nc.sync.dma_start(out=x1_raw[:, FIRST:NCH, :], in_=x1_view[:, FIRST:NCH, :])
-        interleave_w(1, True, True)
-        load_w(4)
-        nc.sync.dma_start(out=x2_raw[:], in_=input2.rearrange("b (h p) i -> p (b h) i", p=P))
-        quant_w(0)
-        quant_tokens(x1_g, x1_c, x1_s, 0, FIRST)
-        interleave_w(2, True, True)
-        load_w(5)
+        nc.vector.tensor_tensor(out=sel[:], in0=ident[:, 0:O], in1=ident[:, O:2 * O], op=ADD)
+        nc.vector.tensor_copy(
+            out=rmat[:].rearrange("p (y o) -> p y o", o=O), in_=sel[:].unsqueeze(1).to_broadcast([P, L, O]))
+        nc.sync.dma_start(out=rmat[2 * O:2 * O + B, :], in_=aff2.rearrange("b y o -> b (y o)"))
+        load_w(2)
+        for b in range(B):
+            nc.vector.memset(a1pad[:, 2 * b:2 * b + 2, 2 * O + b:2 * O + b + 1], 1.0)
 
-        aff2_row = [0]
+        interleave_w(0)
+        nc.sync.dma_start(out=x1_raw[:, FIRST:NCH, :], in_=x1_view[:, FIRST:NCH, :])
+        prep_x1(0, FIRST, nc.scalar.copy)
+        nc.vector.tensor_copy(out=a1pad[:, :, 0:O], in_=a1_raw[:])
+        nc.vector.tensor_copy(
+            out=a1pad[:, :, O:2 * O],
+            in_=bias_bc[:].unsqueeze(1).to_broadcast([P, NCH, O]),
+        )
+        quant_w(0)
+        lt = psum_o.tile([P, NCH, P], BF16, name="lt", tag="o")
+        for c in range(NCH):
+            nc.tensor.transpose(lt[:, c, :], a1pad[:, c, :], ident[:])
+        nc.scalar.copy(out=lmat[:], in_=lt[:])
+        affine_banks(C_HEAD)
+        quant_tokens(x1_g, x1_c, x1_s, 0, FIRST)
+        interleave_w(1)
+        nc.sync.dma_start(out=x2_raw[:], in_=input2.rearrange("b (h p) i -> p (b h) i", p=P))
+        interleave_w(2)
+
         jobs = [(c, g, yh) for c in range(NCH) for g in range(NG) for yh in range(2)]
         for k in range(len(W_GROUPS)):
-            interleave_w(k + 3, False, True)
             quant_w(k + 1)
-            interleave_w(k + 3, True, False)
-            load_w(k + 3 + W_PREFETCH)
-            if k == 1:
-                nc.vector.tensor_copy(out=a2_perm[:], in_=a2_rows[:].rearrange("p y o -> p o y"))
+            interleave_w(k + 3)
             if k == 3:
                 nc.vector.tensor_copy(
                     out=x2_perm[:].rearrange("p c t (a i) -> p c t a i", i=4),
@@ -295,7 +269,7 @@ def tile_biaffine_2_pa_kernel(tc, input1, input2, w1, aff1, aff2, bias, out):
                 for c in range(FIRST):
                     quant_u(c, (k - 3) // 2)
             if k == len(W_GROUPS) - 1:
-                early = {job: stage2(*job) for job in jobs[0:4]}
+                early = {job: stage2(*job) for job in jobs[0:EARLY]}
             for o in W_GROUPS[k]:
                 for c in range(FIRST):
                     take_u(c, o, first_product(c, o), nc.scalar.copy)
@@ -308,20 +282,12 @@ def tile_biaffine_2_pa_kernel(tc, input1, input2, w1, aff1, aff2, bias, out):
                     prep_x2(c)
             if k == 5:
                 quant_tokens(x2_g, x2_c, x2_s, 0, NCH)
-            if k in (2, 5, 6, 7):
-                for r in range(2):
-                    spread_aff2(aff2_row[0])
-                    aff2_row[0] += 1
-        nc.vector.tensor_tensor(
-            out=a1b[:], in0=a1_raw[:], in1=bias_bc[:].unsqueeze(1).to_broadcast([P, NCH, O]), op=ADD)
+            affine_banks(C_HEAD + C_STEP * (k + 1))
 
         last = NCH * NG - 1
-        done = 0
-        for i in range(4):
-            affine(i)
-        for job in jobs[0:4]:
+        for job in jobs[0:EARLY]:
             final_add(*job, early[job])
-        done = 4
+        done = EARLY
         for c in range(FIRST):
             quant_u(c, NG - 1)
         for s in range(FIRST * NG, NCH * NG):
@@ -330,21 +296,19 @@ def tile_biaffine_2_pa_kernel(tc, input1, input2, w1, aff1, aff2, bias, out):
                 quant_u(*groups[s - 1])
             upto = min(done + 4, 2 * (s - 1))
             now = jobs[done:upto]
-            banks = []
             for i in range(QG):
                 if i < len(now):
-                    banks.append(stage2(*now[i]))
+                    pb = stage2(*now[i])
                 ub = first_product(c, QG * g + i)
                 if i == QG - 1 and s >= V_EVAC_FROM:
                     late = ub
                 else:
                     take_u(c, QG * g + i, ub, nc.scalar.copy)
-            for i in range(len(now)):
-                final_add(*now[i], banks[i])
+                if i < len(now):
+                    final_add(*now[i], pb)
             if s >= V_EVAC_FROM:
                 take_u(c, QG * g + QG - 1, late, nc.vector.tensor_copy)
-            affine(4 + 2 * (s - FIRST * NG))
-            affine(5 + 2 * (s - FIRST * NG))
+            affine_banks(C_HEAD + C_STEP * (len(W_GROUPS) + s - FIRST * NG + 1))
             done = upto
         quant_u(*groups[last])
         for yh in range(2):

@@ -19,7 +19,7 @@ NTOK = B * L
 QG = 4
 NG = O // QG
 EARLY = 3
-V_EVAC_FROM = 14
+V_EVAC_FROM = 12
 LAST_SPLIT = 2
 C_HEAD = 4
 C_STEP = 2
@@ -256,7 +256,8 @@ def tile_biaffine_2_pa_kernel(tc, input1, input2, w1, aff1, aff2, bias, out):
         nc.sync.dma_start(out=x2_raw[:], in_=input2.rearrange("b (h p) i -> p (b h) i", p=P))
         interleave_w(2)
 
-        jobs = [(c, g, yh) for c in range(NCH) for g in range(NG) for yh in range(2)]
+        jobs = [(c, g, yh) for c in range(NCH - 1) for g in range(NG) for yh in range(2)]
+        jobs = jobs + [(NCH - 1, g, yh) for yh in range(2) for g in range(NG)]
         for k in range(len(W_GROUPS)):
             quant_w(k + 1)
             interleave_w(k + 3)
@@ -294,7 +295,9 @@ def tile_biaffine_2_pa_kernel(tc, input1, input2, w1, aff1, aff2, bias, out):
             c, g = divmod(s, NG)
             if s > FIRST * NG:
                 quant_u(*groups[s - 1])
-            upto = min(done + 4, 2 * (s - 1))
+            upto = done
+            while upto < done + QG and NG * jobs[upto][0] + jobs[upto][1] < s - 1:
+                upto = upto + 1
             now = jobs[done:upto]
             for i in range(QG):
                 if i < len(now):
@@ -311,7 +314,5 @@ def tile_biaffine_2_pa_kernel(tc, input1, input2, w1, aff1, aff2, bias, out):
             affine_banks(C_HEAD + C_STEP * (len(W_GROUPS) + s - FIRST * NG + 1))
             done = upto
         quant_u(*groups[last])
-        for yh in range(2):
-            tail = [(NCH - 1, g, yh) for g in range(NG) if (NCH - 1, g, yh) in jobs[done:]]
-            for job in tail:
-                final_add(*job, stage2(*job), LAST_SPLIT if job == jobs[-1] else 1)
+        for job in jobs[done:]:
+            final_add(*job, stage2(*job), LAST_SPLIT if job[1] == NG - 1 else 1)

@@ -19,9 +19,10 @@ NTOK = B * L
 QG = 4
 NG = O // QG
 EARLY = 3
+V_BRIDGE = 2
 V_EVAC_FROM = 12
 LAST_SPLIT = 2
-C_HEAD = 4
+C_HEAD = 6
 C_STEP = 2
 FIRST = 2
 FLOPS = 2 * (B * L) * D * (O * D) + 2 * B * (L * O) * D * L
@@ -271,9 +272,14 @@ def tile_biaffine_2_pa_kernel(tc, input1, input2, w1, aff1, aff2, bias, out):
                     quant_u(c, (k - 3) // 2)
             if k == len(W_GROUPS) - 1:
                 early = {job: stage2(*job) for job in jobs[0:EARLY]}
+            held = []
             for o in W_GROUPS[k]:
                 for c in range(FIRST):
-                    take_u(c, o, first_product(c, o), nc.scalar.copy)
+                    ub = first_product(c, o)
+                    if k == len(W_GROUPS) - 1 and c == 1 and o >= O - V_BRIDGE:
+                        held.append((c, o, ub))
+                    else:
+                        take_u(c, o, ub, nc.scalar.copy)
             if k == 2:
                 prep_x1(FIRST, NCH, nc.scalar.copy)
             if k == 3:
@@ -289,6 +295,8 @@ def tile_biaffine_2_pa_kernel(tc, input1, input2, w1, aff1, aff2, bias, out):
         for job in jobs[0:EARLY]:
             final_add(*job, early[job])
         done = EARLY
+        for c, o, ub in held:
+            take_u(c, o, ub, nc.vector.tensor_copy)
         for c in range(FIRST):
             quant_u(c, NG - 1)
         for s in range(FIRST * NG, NCH * NG):

from contextlib import ExitStack

import concourse.mybir as mybir
from concourse.masks import make_identity

F32 = mybir.dt.float32
BF16 = mybir.dt.bfloat16
U32 = mybir.dt.uint32
U8 = mybir.dt.uint8
I32 = mybir.dt.int32
FP8X4 = mybir.dt.float8_e4m3fn_x4
ADD = mybir.AluOpType.add

B, L, D, O = 2, 256, 512, 16
P = 128
PACK = 4
NCH = (B * L) // P
NTOK = B * L
QG = 4
NG = O // QG
EARLY = 3
V_BRIDGE = 2
V_EVAC_FROM = 12
LAST_SPLIT = 2
C_HEAD = 6
C_STEP = 2
FIRST = 2
FLOPS = 2 * (B * L) * D * (O * D) + 2 * B * (L * O) * D * L

W_GROUPS = [[0], [1]] + [[o, o + 1] for o in range(2, O, 2)]
W_PREFETCH = 3


def tile_biaffine_2_pa_kernel(tc, input1, input2, w1, aff1, aff2, bias, out):
    nc = tc.nc
    with ExitStack() as ctx:
        const = ctx.enter_context(tc.tile_pool(name="const", bufs=1))
        wraw_pool = ctx.enter_context(tc.tile_pool(name="wraw", bufs=W_PREFETCH))
        wg_pool = ctx.enter_context(tc.tile_pool(name="wg", bufs=3))
        ug_pool = ctx.enter_context(tc.tile_pool(name="ug", bufs=4))
        uq_pool = ctx.enter_context(tc.tile_pool(name="uq", bufs=8))
        psum_u = ctx.enter_context(tc.psum_pool(name="psumu", bufs=3))
        psum_o = ctx.enter_context(tc.psum_pool(name="psumo", bufs=3))
        psum_c = ctx.enter_context(tc.psum_pool(name="psumc", bufs=2))
        ctx.enter_context(tc.manual_schedule())

        ident_f = const.tile([P, P], F32)
        ident = const.tile([P, P], BF16)
        a1_raw = const.tile([P, NCH, O], BF16)
        a1pad = const.tile([P, NCH, P], BF16)
        bias_bc = const.tile([P, O], BF16)
        sel = const.tile([P, O], BF16)
        rmat = const.tile([P, L * O], BF16)
        lmat = const.tile([P, NCH, P], BF16)
        x1_raw = const.tile([P, NCH, D], BF16)
        x2_raw = const.tile([P, NCH, D], BF16)
        x2_perm = const.tile([P, NCH, PACK, P], BF16)
        x1_g = const.tile([P, NTOK, PACK], BF16, align_bytes=64)
        x2_g = const.tile([P, NTOK, PACK], BF16, align_bytes=64)
        x1_c = const.tile([P, NTOK], U32, align_bytes=64)
        x1_s = const.tile([P, NTOK], U8, align_bytes=64)
        x2_c = const.tile([P, NTOK], U32, align_bytes=64)
        x2_s = const.tile([P, NTOK], U8, align_bytes=64)
        w_c = const.tile([P, O * D], U32, align_bytes=64)
        w_s = const.tile([P, O * D], U8, align_bytes=64)
        osb = [const.tile([P, L, O], F32, name="osb%d" % c) for c in range(NCH)]

        w_view = w1.rearrange("(p k) o j -> p k o j", k=PACK)
        w_raw = {}
        w_g = {}
        u_g = {}
        u_q = {}
        w_group_of = {}
        for k in range(len(W_GROUPS)):
            for o in W_GROUPS[k]:
                w_group_of[o] = k

        def load_w(k):
            if k >= len(W_GROUPS):
                return
            n = len(W_GROUPS[k])
            o0 = W_GROUPS[k][0]
            wr = wraw_pool.tile([P, PACK, 2, D], BF16, name="wr", tag="wr")
            nc.sync.dma_start(out=wr[:, :, 0:n, :], in_=w_view[:, :, o0:o0 + n, :])
            w_raw[k] = wr

        def interleave_w(k):
            if k >= len(W_GROUPS):
                return
            n = len(W_GROUPS[k])
            w_g[k] = wg_pool.tile([P, 2 * D, PACK], BF16, name="wg", tag="wg", align_bytes=64)
            nc.vector.tensor_copy(
                out=w_g[k][:, 0:n * D, :].rearrange("p (t x i) k -> p x t k i", t=PACK, i=4),
                in_=w_raw[k][:, :, 0:n, :].rearrange("p k n (a t i) -> p k (n a) t i", t=PACK, i=4).rearrange(
                    "p k x t i -> p x t k i"),
            )
            load_w(k + W_PREFETCH)

        def quant_w(k):
            if k >= len(W_GROUPS):
                return
            n = len(W_GROUPS[k])
            c0 = W_GROUPS[k][0] * D
            nc.vector.quantize_mx(
                out=w_c[:, c0:c0 + n * D].bitcast(FP8X4),
                scales=w_s[:, c0:c0 + n * D],
                in_=w_g[k][:, 0:n * D, :].rearrange("p c t -> p (c t)"),
            )

        def prep_x1(c0, c1, copy):
            xt = psum_o.tile([P, c1 - c0, 2, P], F32, name="xt", tag="o")
            for c in range(c0, c1):
                words = x1_raw[:, c, :].bitcast(F32)
                for u in range(2):
                    nc.tensor.transpose(xt[:, c - c0, u, :], words[:, u:D // 2:2], ident_f[:])
            copy(
                out=x1_g[:, c0 * P:c1 * P, :].bitcast(F32).rearrange("p (c r) u -> p c r u", r=P),
                in_=xt[:].rearrange("p c u r -> p c r u"),
            )

        def prep_x2(c):
            xt = psum_o.tile([P, PACK, P], BF16, name="xt2", tag="o")
            for t in range(PACK):
                nc.tensor.transpose(xt[:, t, :], x2_perm[:, c, t, :], ident[:])
            nc.scalar.copy(
                out=x2_g[:, c * P:(c + 1) * P, :],
                in_=xt[:].rearrange("p t r -> p r t"),
            )

        def quant_tokens(grouped, codes, scales, c0, c1):
            nc.vector.quantize_mx(
                out=codes[:, c0 * P:c1 * P].bitcast(FP8X4),
                scales=scales[:, c0 * P:c1 * P],
                in_=grouped[:, c0 * P:c1 * P, :].rearrange("p r t -> p (r t)"),
            )

        def first_product(c, o):
            k = w_group_of[o]
            n = len(W_GROUPS[k])
            base = W_GROUPS[k][0] * D + (o - W_GROUPS[k][0]) * P
            ub = psum_u.tile([P, PACK, P], F32, name="ub", tag="u")
            for t in range(PACK):
                w0 = base + t * n * P
                nc.tensor.matmul_mx(
                    out=ub[:, t, :],
                    lhsT=w_c[:, w0:w0 + P].bitcast(FP8X4),
                    lhsT_scale=w_s[:, w0:w0 + P],
                    rhs=x1_c[:, c * P:(c + 1) * P].bitcast(FP8X4),
                    rhs_scale=x1_s[:, c * P:(c + 1) * P],
                    start=True,
                    stop=True,
                )
            return ub

        def take_u(c, o, ub, copy):
            g, oo = divmod(o, QG)
            if oo == 0:
                u_g[(c, g)] = ug_pool.tile([P, QG * P, PACK], BF16, name="ug", tag="ug", align_bytes=64)
            copy(
                out=u_g[(c, g)][:, oo * P:(oo + 1) * P, :],
                in_=ub[:].rearrange("p t r -> p r t"),
            )

        def quant_u(c, g):
            uc = uq_pool.tile([P, QG * P], U32, name="uc", tag="uc", align_bytes=64)
            us = uq_pool.tile([P, QG * P], U8, name="us", tag="us", align_bytes=64)
            nc.vector.quantize_mx(
                out=uc[:].bitcast(FP8X4),
                scales=us[:],
                in_=u_g[(c, g)][:].rearrange("p r t -> p (r t)"),
            )
            u_q[(c, g)] = (uc, us)

        groups = [(c, g) for c in range(NCH) for g in range(NG)]
        affine_done = [0]

        def affine_banks(upto):
            while affine_done[0] < min(upto, NCH * 8):
                c, s = divmod(affine_done[0], 8)
                affine_done[0] = affine_done[0] + 1
                cb = psum_c.tile([P, 32, O], F32, name="cb", tag="cb")
                nc.tensor.matmul(
                    out=cb[:],
                    lhsT=lmat[:, c, :],
                    rhs=rmat[:, s * 512:(s + 1) * 512],
                    start=True,
                    stop=True,
                )
                nc.scalar.copy(out=osb[c][:, s * 32:(s + 1) * 32, :], in_=cb[:])

        def stage2(c, g, yh):
            uc, us = u_q[(c, g)]
            c2 = 2 * (c // 2) + yh
            pb = psum_o.tile([P, QG, P], F32, name="pb", tag="o")
            for oo in range(QG):
                nc.tensor.matmul_mx(
                    out=pb[:, oo, :],
                    lhsT=uc[:, oo * P:(oo + 1) * P].bitcast(FP8X4),
                    lhsT_scale=us[:, oo * P:(oo + 1) * P],
                    rhs=x2_c[:, c2 * P:(c2 + 1) * P].bitcast(FP8X4),
                    rhs_scale=x2_s[:, c2 * P:(c2 + 1) * P],
                    start=True,
                    stop=True,
                )
            return pb

        def final_add(c, g, yh, pb, pieces=1):
            ob = osb[c][:, yh * P:(yh + 1) * P, :]
            step = P // pieces
            for y0 in range(0, P, step):
                nc.vector.tensor_tensor(
                    out=ob[:, y0:y0 + step, QG * g:QG * (g + 1)],
                    in0=pb[:, :, y0:y0 + step].rearrange("p o y -> p y o"),
                    in1=ob[:, y0:y0 + step, QG * g:QG * (g + 1)],
                    op=ADD,
                )
                if g == NG - 1:
                    b, h = divmod(c, 2)
                    nc.sync.dma_start(
                        out=out[b, h * P:(h + 1) * P, yh * P + y0:yh * P + y0 + step, :],
                        in_=ob[:, y0:y0 + step, :],
                    )

        make_identity(nc, ident_f[:])
        x1_view = input1.rearrange("b (h p) i -> p (b h) i", p=P)
        nc.scalar.dma_start(out=a1_raw[:], in_=aff1.rearrange("b (h p) o -> p (b h) o", p=P))
        nc.scalar.dma_start(out=bias_bc[:], in_=bias.partition_broadcast(P))
        load_w(0)
        nc.sync.dma_start(out=x1_raw[:, 0:FIRST, :], in_=x1_view[:, 0:FIRST, :])
        load_w(1)
        nc.vector.memset(a1pad[:].bitcast(I32), 0)
        nc.vector.tensor_copy(out=ident[:], in_=ident_f[:])
        nc.vector.tensor_tensor(out=sel[:], in0=ident[:, 0:O], in1=ident[:, O:2 * O], op=ADD)
        nc.vector.tensor_copy(
            out=rmat[:].rearrange("p (y o) -> p y o", o=O), in_=sel[:].unsqueeze(1).to_broadcast([P, L, O]))
        nc.sync.dma_start(out=rmat[2 * O:2 * O + B, :], in_=aff2.rearrange("b y o -> b (y o)"))
        load_w(2)
        for b in range(B):
            nc.vector.memset(a1pad[:, 2 * b:2 * b + 2, 2 * O + b:2 * O + b + 1], 1.0)

        interleave_w(0)
        nc.sync.dma_start(out=x1_raw[:, FIRST:NCH, :], in_=x1_view[:, FIRST:NCH, :])
        prep_x1(0, FIRST, nc.scalar.copy)
        nc.vector.tensor_copy(out=a1pad[:, :, 0:O], in_=a1_raw[:])
        nc.vector.tensor_copy(
            out=a1pad[:, :, O:2 * O],
            in_=bias_bc[:].unsqueeze(1).to_broadcast([P, NCH, O]),
        )
        quant_w(0)
        lt = psum_o.tile([P, NCH, P], BF16, name="lt", tag="o")
        for c in range(NCH):
            nc.tensor.transpose(lt[:, c, :], a1pad[:, c, :], ident[:])
        nc.scalar.copy(out=lmat[:], in_=lt[:])
        affine_banks(C_HEAD)
        quant_tokens(x1_g, x1_c, x1_s, 0, FIRST)
        interleave_w(1)
        nc.sync.dma_start(out=x2_raw[:], in_=input2.rearrange("b (h p) i -> p (b h) i", p=P))
        interleave_w(2)

        jobs = [(c, g, yh) for c in range(NCH - 1) for g in range(NG) for yh in range(2)]
        jobs = jobs + [(NCH - 1, g, yh) for yh in range(2) for g in range(NG)]
        for k in range(len(W_GROUPS)):
            quant_w(k + 1)
            interleave_w(k + 3)
            if k == 3:
                nc.vector.tensor_copy(
                    out=x2_perm[:].rearrange("p c t (a i) -> p c t a i", i=4),
                    in_=x2_raw[:].rearrange("p c (a t i) -> p c t a i", t=PACK, i=4),
                )
            if k in (3, 5, 7):
                for c in range(FIRST):
                    quant_u(c, (k - 3) // 2)
            if k == len(W_GROUPS) - 1:
                early = {job: stage2(*job) for job in jobs[0:EARLY]}
            held = []
            for o in W_GROUPS[k]:
                for c in range(FIRST):
                    ub = first_product(c, o)
                    if k == len(W_GROUPS) - 1 and c == 1 and o >= O - V_BRIDGE:
                        held.append((c, o, ub))
                    else:
                        take_u(c, o, ub, nc.scalar.copy)
            if k == 2:
                prep_x1(FIRST, NCH, nc.scalar.copy)
            if k == 3:
                quant_tokens(x1_g, x1_c, x1_s, FIRST, NCH)
            if k == 4:
                for c in range(NCH):
                    prep_x2(c)
            if k == 5:
                quant_tokens(x2_g, x2_c, x2_s, 0, NCH)
            affine_banks(C_HEAD + C_STEP * (k + 1))

        last = NCH * NG - 1
        for job in jobs[0:EARLY]:
            final_add(*job, early[job])
        done = EARLY
        for c, o, ub in held:
            take_u(c, o, ub, nc.vector.tensor_copy)
        for c in range(FIRST):
            quant_u(c, NG - 1)
        for s in range(FIRST * NG, NCH * NG):
            c, g = divmod(s, NG)
            if s > FIRST * NG:
                quant_u(*groups[s - 1])
            upto = done
            while upto < done + QG and NG * jobs[upto][0] + jobs[upto][1] < s - 1:
                upto = upto + 1
            now = jobs[done:upto]
            for i in range(QG):
                if i < len(now):
                    pb = stage2(*now[i])
                ub = first_product(c, QG * g + i)
                if i == QG - 1 and s >= V_EVAC_FROM:
                    late = ub
                else:
                    take_u(c, QG * g + i, ub, nc.scalar.copy)
                if i < len(now):
                    final_add(*now[i], pb)
            if s >= V_EVAC_FROM:
                take_u(c, QG * g + QG - 1, late, nc.vector.tensor_copy)
            affine_banks(C_HEAD + C_STEP * (len(W_GROUPS) + s - FIRST * NG + 1))
            done = upto
        quant_u(*groups[last])
        for job in jobs[done:]:
            final_add(*job, stage2(*job), LAST_SPLIT if job[1] == NG - 1 else 1)
